import numpy as np
import ml_dtypes

BF16 = ml_dtypes.bfloat16


def bf(x):
    return np.asarray(x, np.float32).astype(BF16)


def f32(x):
    return np.asarray(x, np.float32)


def f64(x):
    return np.asarray(x).astype(np.float64)


def striped(idx):
    return np.tile(idx.reshape(-1, 16).T, (8, 1))


C, C2, S, M, B, N = 128, 256, 512, 4, 512, 2048
STAB = 10.0
AGES = np.arange(M - 1, -1, -1).astype(np.float64)
WGT = np.exp(-AGES * (AGES + 1.0) / (2.0 * STAB))


def setup_inputs():
    return {"table": f32(np.random.standard_normal((C, S))), "q": bf(np.random.standard_normal((C, B))), "w1": bf(np.random.standard_normal((C2, C)) / np.sqrt(C2)), "b1": f32(0.1 * np.random.standard_normal((C, 1))), "w2": bf(np.random.standard_normal((C, S)) / np.sqrt(C)), "b2": f32(0.1 * np.random.standard_normal((S, 1))), "offs": striped(np.concatenate([np.random.permutation(S) for _ in range(M)]))}


def reference(table, q, w1, b1, w2, b2, offs):
    idx = offs[:16].T.reshape(-1)
    picked = f64(table)[:, idx].reshape(C, M, B)
    mem = (picked * WGT[None, :, None]).sum(axis=1) / M
    h0 = np.concatenate([f64(q), mem], axis=0)
    hid = np.maximum(f64(w1).T @ h0 + f64(b1), 0.0)
    return f64(w2).T @ hid + f64(b2)

@@ -1,0 +1,88 @@
+import math
+from contextlib import ExitStack
+
+import concourse.mybir as mybir
+
+F32, BF16, U16 = mybir.dt.float32, mybir.dt.bfloat16, mybir.dt.uint16
+MULT, ADD = mybir.AluOpType.mult, mybir.AluOpType.add
+RELU = mybir.ActivationFunctionType.Relu
+IDENTITY = mybir.ActivationFunctionType.Identity
+COPY = mybir.ActivationFunctionType.Copy
+
+P = 128
+WORDS = 512
+SAMPLES = 512
+SLOTS = 4
+VBLOCKS = 4
+CHUNK = 512
+WGT = [math.exp(-age * (age + 1) / 20.0) for age in (3, 2, 1, 0)]
+
+FLOPS = 2 * 256 * P * SAMPLES + 2 * P * 512 * SAMPLES
+
+
+def tile_ebbinghausmodel_kernel(tc, table, q, w1, b1, w2, b2, offs, out):
+    nc = tc.nc
+    with ExitStack() as ctx:
+        held = ctx.enter_context(tc.tile_pool(name="held", bufs=1))
+        work = ctx.enter_context(tc.tile_pool(name="work", bufs=2))
+        stage = ctx.enter_context(tc.tile_pool(name="stage", bufs=4))
+        psum_hid = ctx.enter_context(tc.psum_pool(name="psum_hid", bufs=2))
+        psum_out = ctx.enter_context(tc.psum_pool(name="psum_out", bufs=4))
+
+        offsets = held.tile([P, SLOTS * SAMPLES // 16], U16, name="offsets")
+        nc.sync.dma_start(offsets[:], offs)
+        table_sb = held.tile([P, WORDS], F32, name="table_sb")
+        nc.scalar.dma_start(table_sb[:], table)
+        q_sb = held.tile([P, SAMPLES], BF16, name="q_sb")
+        nc.sync.dma_start(q_sb[:], q)
+        w1_sb = held.tile([P, 2, P], BF16, name="w1_sb")
+        nc.sync.dma_start(w1_sb[:], w1.rearrange("(half k) d -> k half d", k=P))
+        b1_sb = held.tile([P, 1], F32, name="b1_sb")
+        nc.sync.dma_start(b1_sb[:], b1)
+        w2_sb = held.tile([P, VBLOCKS * P], BF16, name="w2_sb")
+        nc.scalar.dma_start(w2_sb[:], w2)
+        b2_sb = held.tile([P, VBLOCKS], F32, name="b2_sb")
+        with nc.allow_non_contiguous_dma(reason="512 floats, one to a partition and block"):
+            nc.scalar.dma_start(b2_sb[:], b2.rearrange("(v p) one -> p (v one)", p=P))
+
+        decay_older = held.tile([P, CHUNK], F32, name="decay_older")
+        nc.gpsimd.memset(decay_older[:], WGT[0] / WGT[1])
+        decay_newer = held.tile([P, CHUNK], F32, name="decay_newer")
+        nc.gpsimd.memset(decay_newer[:], WGT[2])
+
+        for first in range(0, SAMPLES, CHUNK):
+            picked = []
+            for t in range(SLOTS):
+                column = (t * SAMPLES + first) // 16
+                picked.append(table_sb[:].indirect(offsets[:, column : column + CHUNK // 16]))
+
+            hid_ps = psum_hid.tile([P, CHUNK], F32, name="hid_ps")
+            nc.tensor.matmul(
+                hid_ps[:], w1_sb[:, 0, :], q_sb[:, first : first + CHUNK], start=True, stop=False
+            )
+
+            faded0 = work.tile([P, CHUNK], F32, name="faded0")
+            nc.vector.tensor_tensor(faded0[:], picked[0], decay_older[:], MULT)
+            older = work.tile([P, CHUNK], F32, name="older")
+            nc.vector.tensor_tensor(older[:], picked[1], faded0[:], ADD)
+            older_scaled = work.tile([P, CHUNK], F32, name="older_scaled")
+            nc.scalar.activation(older_scaled[:], older[:], COPY, scale=WGT[1] / SLOTS)
+            faded2 = work.tile([P, CHUNK], F32, name="faded2")
+            nc.vector.tensor_tensor(faded2[:], picked[2], decay_newer[:], MULT)
+            newer = work.tile([P, CHUNK], F32, name="newer")
+            nc.vector.tensor_tensor(newer[:], picked[3], faded2[:], ADD)
+            mem = work.tile([P, CHUNK], BF16, name="mem")
+            nc.vector.scalar_tensor_tensor(
+                mem[:], newer[:], 1.0 / SLOTS, older_scaled[:], op0=MULT, op1=ADD
+            )
+
+            nc.tensor.matmul(hid_ps[:], w1_sb[:, 1, :], mem[:], start=False, stop=True)
+            hid = work.tile([P, CHUNK], BF16, name="hid")
+            nc.scalar.activation(hid[:], hid_ps[:], RELU, bias=b1_sb[:, 0:1])
+
+            for v in range(VBLOCKS):
+                out_ps = psum_out.tile([P, CHUNK], F32, name="out_ps")
+                nc.tensor.matmul(out_ps[:], w2_sb[:, v * P : (v + 1) * P], hid[:], start=True, stop=True)
+                out_sb = stage.tile([P, CHUNK], F32, name="out_sb")
+                nc.scalar.activation(out_sb[:], out_ps[:], IDENTITY, bias=b2_sb[:, v : v + 1])
+                nc.sync.dma_start(out[v * P : (v + 1) * P, first : first + CHUNK], out_sb[:])

@@ -14,7 +14,7 @@ WORDS = 512
 SAMPLES = 512
 SLOTS = 4
 VBLOCKS = 4
-CHUNK = 512
+CHUNK = 128
 WGT = [math.exp(-age * (age + 1) / 20.0) for age in (3, 2, 1, 0)]
 
 FLOPS = 2 * 256 * P * SAMPLES + 2 * P * 512 * SAMPLES
@@ -25,9 +25,9 @@ def tile_ebbinghausmodel_kernel(tc, table, q, w1, b1, w2, b2, offs, out):
     with ExitStack() as ctx:
         held = ctx.enter_context(tc.tile_pool(name="held", bufs=1))
         work = ctx.enter_context(tc.tile_pool(name="work", bufs=2))
-        stage = ctx.enter_context(tc.tile_pool(name="stage", bufs=4))
+        stage = ctx.enter_context(tc.tile_pool(name="stage", bufs=8))
         psum_hid = ctx.enter_context(tc.psum_pool(name="psum_hid", bufs=2))
-        psum_out = ctx.enter_context(tc.psum_pool(name="psum_out", bufs=4))
+        psum_out = ctx.enter_context(tc.psum_pool(name="psum_out", bufs=6))
 
         offsets = held.tile([P, SLOTS * SAMPLES // 16], U16, name="offsets")
         nc.sync.dma_start(offsets[:], offs)

@@ -14,7 +14,7 @@ WORDS = 512
 SAMPLES = 512
 SLOTS = 4
 VBLOCKS = 4
-CHUNK = 128
+CHUNK = 256
 WGT = [math.exp(-age * (age + 1) / 20.0) for age in (3, 2, 1, 0)]
 
 FLOPS = 2 * 256 * P * SAMPLES + 2 * P * 512 * SAMPLES

@@ -4,17 +4,17 @@ from contextlib import ExitStack
 import concourse.mybir as mybir
 
 F32, BF16, U16 = mybir.dt.float32, mybir.dt.bfloat16, mybir.dt.uint16
-MULT, ADD = mybir.AluOpType.mult, mybir.AluOpType.add
+MULT, ADD, MAX = mybir.AluOpType.mult, mybir.AluOpType.add, mybir.AluOpType.max
 RELU = mybir.ActivationFunctionType.Relu
 IDENTITY = mybir.ActivationFunctionType.Identity
-COPY = mybir.ActivationFunctionType.Copy
 
 P = 128
 WORDS = 512
 SAMPLES = 512
 SLOTS = 4
 VBLOCKS = 4
-CHUNK = 256
+CHUNKS = (256, 256)
+WIDEST = max(CHUNKS)
 WGT = [math.exp(-age * (age + 1) / 20.0) for age in (3, 2, 1, 0)]
 
 FLOPS = 2 * 256 * P * SAMPLES + 2 * P * 512 * SAMPLES
@@ -25,7 +25,7 @@ def tile_ebbinghausmodel_kernel(tc, table, q, w1, b1, w2, b2, offs, out):
     with ExitStack() as ctx:
         held = ctx.enter_context(tc.tile_pool(name="held", bufs=1))
         work = ctx.enter_context(tc.tile_pool(name="work", bufs=2))
-        stage = ctx.enter_context(tc.tile_pool(name="stage", bufs=8))
+        stage = ctx.enter_context(tc.tile_pool(name="stage", bufs=len(CHUNKS) * VBLOCKS))
         psum_hid = ctx.enter_context(tc.psum_pool(name="psum_hid", bufs=2))
         psum_out = ctx.enter_context(tc.psum_pool(name="psum_out", bufs=6))
 
@@ -45,44 +45,47 @@ def tile_ebbinghausmodel_kernel(tc, table, q, w1, b1, w2, b2, offs, out):
         with nc.allow_non_contiguous_dma(reason="512 floats, one to a partition and block"):
             nc.scalar.dma_start(b2_sb[:], b2.rearrange("(v p) one -> p (v one)", p=P))
 
-        decay_older = held.tile([P, CHUNK], F32, name="decay_older")
+        decay_older = held.tile([P, WIDEST], F32, name="decay_older")
         nc.gpsimd.memset(decay_older[:], WGT[0] / WGT[1])
-        decay_newer = held.tile([P, CHUNK], F32, name="decay_newer")
-        nc.gpsimd.memset(decay_newer[:], WGT[2])
+        decay_newer = held.tile([P, WIDEST], F32, name="decay_newer")
+        nc.scalar.mul(decay_newer[:], decay_older[:], WGT[2] * WGT[1] / WGT[0])
+        w1_mem = held.tile([P, P], BF16, name="w1_mem")
+        nc.gpsimd.tensor_scalar_mul(w1_mem[:], w1_sb[:, 1, :], 1.0 / SLOTS)
 
-        for first in range(0, SAMPLES, CHUNK):
+        first = 0
+        for chunk, width in enumerate(CHUNKS):
             picked = []
             for t in range(SLOTS):
                 column = (t * SAMPLES + first) // 16
-                picked.append(table_sb[:].indirect(offsets[:, column : column + CHUNK // 16]))
+                picked.append(table_sb[:].indirect(offsets[:, column : column + width // 16]))
 
-            hid_ps = psum_hid.tile([P, CHUNK], F32, name="hid_ps")
+            hid_ps = psum_hid.tile([P, width], F32, name="hid_ps")
             nc.tensor.matmul(
-                hid_ps[:], w1_sb[:, 0, :], q_sb[:, first : first + CHUNK], start=True, stop=False
+                hid_ps[:], w1_sb[:, 0, :], q_sb[:, first : first + width], start=True, stop=False
             )
 
-            faded0 = work.tile([P, CHUNK], F32, name="faded0")
-            nc.vector.tensor_tensor(faded0[:], picked[0], decay_older[:], MULT)
-            older = work.tile([P, CHUNK], F32, name="older")
+            faded0 = work.tile([P, width], F32, name="faded0")
+            nc.vector.tensor_tensor(faded0[:], picked[0], decay_older[:, :width], MULT)
+            older = work.tile([P, width], F32, name="older")
             nc.vector.tensor_tensor(older[:], picked[1], faded0[:], ADD)
-            older_scaled = work.tile([P, CHUNK], F32, name="older_scaled")
-            nc.scalar.activation(older_scaled[:], older[:], COPY, scale=WGT[1] / SLOTS)
-            faded2 = work.tile([P, CHUNK], F32, name="faded2")
-            nc.vector.tensor_tensor(faded2[:], picked[2], decay_newer[:], MULT)
-            newer = work.tile([P, CHUNK], F32, name="newer")
+            faded2 = work.tile([P, width], F32, name="faded2")
+            nc.vector.tensor_tensor(faded2[:], picked[2], decay_newer[:, :width], MULT)
+            newer = work.tile([P, width], F32, name="newer")
             nc.vector.tensor_tensor(newer[:], picked[3], faded2[:], ADD)
-            mem = work.tile([P, CHUNK], BF16, name="mem")
-            nc.vector.scalar_tensor_tensor(
-                mem[:], newer[:], 1.0 / SLOTS, older_scaled[:], op0=MULT, op1=ADD
-            )
+            mem4 = work.tile([P, width], BF16, name="mem4")
+            nc.vector.scalar_tensor_tensor(mem4[:], older[:], WGT[1], newer[:], op0=MULT, op1=ADD)
 
-            nc.tensor.matmul(hid_ps[:], w1_sb[:, 1, :], mem[:], start=False, stop=True)
-            hid = work.tile([P, CHUNK], BF16, name="hid")
+            nc.tensor.matmul(hid_ps[:], w1_mem[:], mem4[:], start=False, stop=True)
+            hid = work.tile([P, width], BF16, name="hid")
             nc.scalar.activation(hid[:], hid_ps[:], RELU, bias=b1_sb[:, 0:1])
 
             for v in range(VBLOCKS):
-                out_ps = psum_out.tile([P, CHUNK], F32, name="out_ps")
+                out_ps = psum_out.tile([P, width], F32, name="out_ps")
                 nc.tensor.matmul(out_ps[:], w2_sb[:, v * P : (v + 1) * P], hid[:], start=True, stop=True)
-                out_sb = stage.tile([P, CHUNK], F32, name="out_sb")
-                nc.scalar.activation(out_sb[:], out_ps[:], IDENTITY, bias=b2_sb[:, v : v + 1])
-                nc.sync.dma_start(out[v * P : (v + 1) * P, first : first + CHUNK], out_sb[:])
+                out_sb = stage.tile([P, width], F32, name="out_sb")
+                if chunk == len(CHUNKS) - 1 and v % 2 == 1:
+                    nc.vector.tensor_scalar_add(out_sb[:], out_ps[:], b2_sb[:, v : v + 1])
+                else:
+                    nc.scalar.activation(out_sb[:], out_ps[:], IDENTITY, bias=b2_sb[:, v : v + 1])
+                nc.sync.dma_start(out[v * P : (v + 1) * P, first : first + width], out_sb[:])
+            first += width

@@ -13,7 +13,7 @@ WORDS = 512
 SAMPLES = 512
 SLOTS = 4
 VBLOCKS = 4
-CHUNKS = (256, 256)
+CHUNKS = (128, 128, 128, 128)
 WIDEST = max(CHUNKS)
 WGT = [math.exp(-age * (age + 1) / 20.0) for age in (3, 2, 1, 0)]
 

@@ -4,7 +4,7 @@ from contextlib import ExitStack
 import concourse.mybir as mybir
 
 F32, BF16, U16 = mybir.dt.float32, mybir.dt.bfloat16, mybir.dt.uint16
-MULT, ADD, MAX = mybir.AluOpType.mult, mybir.AluOpType.add, mybir.AluOpType.max
+MULT, ADD = mybir.AluOpType.mult, mybir.AluOpType.add
 RELU = mybir.ActivationFunctionType.Relu
 IDENTITY = mybir.ActivationFunctionType.Identity
 
@@ -24,7 +24,7 @@ def tile_ebbinghausmodel_kernel(tc, table, q, w1, b1, w2, b2, offs, out):
     nc = tc.nc
     with ExitStack() as ctx:
         held = ctx.enter_context(tc.tile_pool(name="held", bufs=1))
-        work = ctx.enter_context(tc.tile_pool(name="work", bufs=2))
+        work = ctx.enter_context(tc.tile_pool(name="work", bufs=len(CHUNKS)))
         stage = ctx.enter_context(tc.tile_pool(name="stage", bufs=len(CHUNKS) * VBLOCKS))
         psum_hid = ctx.enter_context(tc.psum_pool(name="psum_hid", bufs=2))
         psum_out = ctx.enter_context(tc.psum_pool(name="psum_out", bufs=6))
@@ -32,25 +32,25 @@ def tile_ebbinghausmodel_kernel(tc, table, q, w1, b1, w2, b2, offs, out):
         offsets = held.tile([P, SLOTS * SAMPLES // 16], U16, name="offsets")
         nc.sync.dma_start(offsets[:], offs)
         table_sb = held.tile([P, WORDS], F32, name="table_sb")
-        nc.scalar.dma_start(table_sb[:], table)
-        q_sb = held.tile([P, SAMPLES], BF16, name="q_sb")
-        nc.sync.dma_start(q_sb[:], q)
+        nc.sync.dma_start(table_sb[:], table)
         w1_sb = held.tile([P, 2, P], BF16, name="w1_sb")
         nc.sync.dma_start(w1_sb[:], w1.rearrange("(half k) d -> k half d", k=P))
+        q_sb = held.tile([P, SAMPLES], BF16, name="q_sb")
+        nc.sync.dma_start(q_sb[:], q)
         b1_sb = held.tile([P, 1], F32, name="b1_sb")
         nc.sync.dma_start(b1_sb[:], b1)
         w2_sb = held.tile([P, VBLOCKS * P], BF16, name="w2_sb")
-        nc.scalar.dma_start(w2_sb[:], w2)
+        nc.sync.dma_start(w2_sb[:], w2)
         b2_sb = held.tile([P, VBLOCKS], F32, name="b2_sb")
         with nc.allow_non_contiguous_dma(reason="512 floats, one to a partition and block"):
-            nc.scalar.dma_start(b2_sb[:], b2.rearrange("(v p) one -> p (v one)", p=P))
+            nc.sync.dma_start(b2_sb[:], b2.rearrange("(v p) one -> p (v one)", p=P))
 
         decay_older = held.tile([P, WIDEST], F32, name="decay_older")
         nc.gpsimd.memset(decay_older[:], WGT[0] / WGT[1])
         decay_newer = held.tile([P, WIDEST], F32, name="decay_newer")
-        nc.scalar.mul(decay_newer[:], decay_older[:], WGT[2] * WGT[1] / WGT[0])
+        nc.gpsimd.memset(decay_newer[:], WGT[2])
         w1_mem = held.tile([P, P], BF16, name="w1_mem")
-        nc.gpsimd.tensor_scalar_mul(w1_mem[:], w1_sb[:, 1, :], 1.0 / SLOTS)
+        nc.scalar.mul(w1_mem[:], w1_sb[:, 1, :], 1.0 / SLOTS)
 
         first = 0
         for chunk, width in enumerate(CHUNKS):
@@ -66,10 +66,10 @@ def tile_ebbinghausmodel_kernel(tc, table, q, w1, b1, w2, b2, offs, out):
 
             faded0 = work.tile([P, width], F32, name="faded0")
             nc.vector.tensor_tensor(faded0[:], picked[0], decay_older[:, :width], MULT)
-            older = work.tile([P, width], F32, name="older")
-            nc.vector.tensor_tensor(older[:], picked[1], faded0[:], ADD)
             faded2 = work.tile([P, width], F32, name="faded2")
             nc.vector.tensor_tensor(faded2[:], picked[2], decay_newer[:, :width], MULT)
+            older = work.tile([P, width], F32, name="older")
+            nc.vector.tensor_tensor(older[:], picked[1], faded0[:], ADD)
             newer = work.tile([P, width], F32, name="newer")
             nc.vector.tensor_tensor(newer[:], picked[3], faded2[:], ADD)
             mem4 = work.tile([P, width], BF16, name="mem4")

@@ -13,9 +13,11 @@ WORDS = 512
 SAMPLES = 512
 SLOTS = 4
 VBLOCKS = 4
-CHUNKS = (128, 128, 128, 128)
-WIDEST = max(CHUNKS)
 WGT = [math.exp(-age * (age + 1) / 20.0) for age in (3, 2, 1, 0)]
+
+CHUNKS = (256, 160, 96)
+WIDEST = max(CHUNKS)
+assert sum(CHUNKS) == SAMPLES
 
 FLOPS = 2 * 256 * P * SAMPLES + 2 * P * 512 * SAMPLES
 
@@ -52,40 +54,44 @@ def tile_ebbinghausmodel_kernel(tc, table, q, w1, b1, w2, b2, offs, out):
         w1_mem = held.tile([P, P], BF16, name="w1_mem")
         nc.scalar.mul(w1_mem[:], w1_sb[:, 1, :], 1.0 / SLOTS)
 
+        def network(first, width, older, newer, is_last):
+            hid_ps = psum_hid.tile([P, width], F32, name="hid_ps")
+            nc.tensor.matmul(
+                hid_ps[:], w1_sb[:, 0, :], q_sb[:, first : first + width], start=True, stop=False
+            )
+            mem4 = work.tile([P, width], BF16, name="mem4")
+            nc.vector.scalar_tensor_tensor(mem4[:], older[:], WGT[1], newer[:], op0=MULT, op1=ADD)
+            nc.tensor.matmul(hid_ps[:], w1_mem[:], mem4[:], start=False, stop=True)
+            hid = work.tile([P, width], BF16, name="hid")
+            nc.scalar.activation(hid[:], hid_ps[:], RELU, bias=b1_sb[:, 0:1])
+            for v in range(VBLOCKS):
+                out_ps = psum_out.tile([P, width], F32, name="out_ps")
+                nc.tensor.matmul(out_ps[:], w2_sb[:, v * P : (v + 1) * P], hid[:], start=True, stop=True)
+                out_sb = stage.tile([P, width], F32, name="out_sb")
+                if is_last and v % 2 == 1:
+                    nc.vector.tensor_scalar_add(out_sb[:], out_ps[:], b2_sb[:, v : v + 1])
+                else:
+                    nc.scalar.activation(out_sb[:], out_ps[:], IDENTITY, bias=b2_sb[:, v : v + 1])
+                nc.sync.dma_start(out[v * P : (v + 1) * P, first : first + width], out_sb[:])
+
+        waiting = None
         first = 0
-        for chunk, width in enumerate(CHUNKS):
+        for width in CHUNKS:
             picked = []
             for t in range(SLOTS):
                 column = (t * SAMPLES + first) // 16
                 picked.append(table_sb[:].indirect(offsets[:, column : column + width // 16]))
 
-            hid_ps = psum_hid.tile([P, width], F32, name="hid_ps")
-            nc.tensor.matmul(
-                hid_ps[:], w1_sb[:, 0, :], q_sb[:, first : first + width], start=True, stop=False
-            )
-
             faded0 = work.tile([P, width], F32, name="faded0")
             nc.vector.tensor_tensor(faded0[:], picked[0], decay_older[:, :width], MULT)
+            if waiting is not None:
+                network(*waiting, is_last=False)
             faded2 = work.tile([P, width], F32, name="faded2")
             nc.vector.tensor_tensor(faded2[:], picked[2], decay_newer[:, :width], MULT)
             older = work.tile([P, width], F32, name="older")
             nc.vector.tensor_tensor(older[:], picked[1], faded0[:], ADD)
             newer = work.tile([P, width], F32, name="newer")
             nc.vector.tensor_tensor(newer[:], picked[3], faded2[:], ADD)
-            mem4 = work.tile([P, width], BF16, name="mem4")
-            nc.vector.scalar_tensor_tensor(mem4[:], older[:], WGT[1], newer[:], op0=MULT, op1=ADD)
-
-            nc.tensor.matmul(hid_ps[:], w1_mem[:], mem4[:], start=False, stop=True)
-            hid = work.tile([P, width], BF16, name="hid")
-            nc.scalar.activation(hid[:], hid_ps[:], RELU, bias=b1_sb[:, 0:1])
-
-            for v in range(VBLOCKS):
-                out_ps = psum_out.tile([P, width], F32, name="out_ps")
-                nc.tensor.matmul(out_ps[:], w2_sb[:, v * P : (v + 1) * P], hid[:], start=True, stop=True)
-                out_sb = stage.tile([P, width], F32, name="out_sb")
-                if chunk == len(CHUNKS) - 1 and v % 2 == 1:
-                    nc.vector.tensor_scalar_add(out_sb[:], out_ps[:], b2_sb[:, v : v + 1])
-                else:
-                    nc.scalar.activation(out_sb[:], out_ps[:], IDENTITY, bias=b2_sb[:, v : v + 1])
-                nc.sync.dma_start(out[v * P : (v + 1) * P, first : first + width], out_sb[:])
+            waiting = (first, width, older, newer)
             first += width
+        network(*waiting, is_last=True)

@@ -6,7 +6,6 @@ import concourse.mybir as mybir
 F32, BF16, U16 = mybir.dt.float32, mybir.dt.bfloat16, mybir.dt.uint16
 MULT, ADD = mybir.AluOpType.mult, mybir.AluOpType.add
 RELU = mybir.ActivationFunctionType.Relu
-IDENTITY = mybir.ActivationFunctionType.Identity
 
 P = 128
 WORDS = 512
@@ -15,9 +14,8 @@ SLOTS = 4
 VBLOCKS = 4
 WGT = [math.exp(-age * (age + 1) / 20.0) for age in (3, 2, 1, 0)]
 
-CHUNKS = (256, 160, 96)
-WIDEST = max(CHUNKS)
-assert sum(CHUNKS) == SAMPLES
+CHUNK = 128
+CHUNKS = SAMPLES // CHUNK
 
 FLOPS = 2 * 256 * P * SAMPLES + 2 * P * 512 * SAMPLES
 
@@ -26,8 +24,7 @@ def tile_ebbinghausmodel_kernel(tc, table, q, w1, b1, w2, b2, offs, out):
     nc = tc.nc
     with ExitStack() as ctx:
         held = ctx.enter_context(tc.tile_pool(name="held", bufs=1))
-        work = ctx.enter_context(tc.tile_pool(name="work", bufs=len(CHUNKS)))
-        stage = ctx.enter_context(tc.tile_pool(name="stage", bufs=len(CHUNKS) * VBLOCKS))
+        work = ctx.enter_context(tc.tile_pool(name="work", bufs=CHUNKS))
         psum_hid = ctx.enter_context(tc.psum_pool(name="psum_hid", bufs=2))
         psum_out = ctx.enter_context(tc.psum_pool(name="psum_out", bufs=6))
 
@@ -46,52 +43,47 @@ def tile_ebbinghausmodel_kernel(tc, table, q, w1, b1, w2, b2, offs, out):
         b2_sb = held.tile([P, VBLOCKS], F32, name="b2_sb")
         with nc.allow_non_contiguous_dma(reason="512 floats, one to a partition and block"):
             nc.sync.dma_start(b2_sb[:], b2.rearrange("(v p) one -> p (v one)", p=P))
+        out_blocks = out.rearrange("(v p) n -> p v n", p=P)
 
-        decay_older = held.tile([P, WIDEST], F32, name="decay_older")
+        decay_older = held.tile([P, CHUNK], F32, name="decay_older")
         nc.gpsimd.memset(decay_older[:], WGT[0] / WGT[1])
-        decay_newer = held.tile([P, WIDEST], F32, name="decay_newer")
+        decay_newer = held.tile([P, CHUNK], F32, name="decay_newer")
         nc.gpsimd.memset(decay_newer[:], WGT[2])
         w1_mem = held.tile([P, P], BF16, name="w1_mem")
         nc.scalar.mul(w1_mem[:], w1_sb[:, 1, :], 1.0 / SLOTS)
 
-        def network(first, width, older, newer, is_last):
-            hid_ps = psum_hid.tile([P, width], F32, name="hid_ps")
-            nc.tensor.matmul(
-                hid_ps[:], w1_sb[:, 0, :], q_sb[:, first : first + width], start=True, stop=False
-            )
-            mem4 = work.tile([P, width], BF16, name="mem4")
-            nc.vector.scalar_tensor_tensor(mem4[:], older[:], WGT[1], newer[:], op0=MULT, op1=ADD)
-            nc.tensor.matmul(hid_ps[:], w1_mem[:], mem4[:], start=False, stop=True)
-            hid = work.tile([P, width], BF16, name="hid")
-            nc.scalar.activation(hid[:], hid_ps[:], RELU, bias=b1_sb[:, 0:1])
-            for v in range(VBLOCKS):
-                out_ps = psum_out.tile([P, width], F32, name="out_ps")
-                nc.tensor.matmul(out_ps[:], w2_sb[:, v * P : (v + 1) * P], hid[:], start=True, stop=True)
-                out_sb = stage.tile([P, width], F32, name="out_sb")
-                if is_last and v % 2 == 1:
-                    nc.vector.tensor_scalar_add(out_sb[:], out_ps[:], b2_sb[:, v : v + 1])
-                else:
-                    nc.scalar.activation(out_sb[:], out_ps[:], IDENTITY, bias=b2_sb[:, v : v + 1])
-                nc.sync.dma_start(out[v * P : (v + 1) * P, first : first + width], out_sb[:])
-
-        waiting = None
-        first = 0
-        for width in CHUNKS:
+        for first in range(0, SAMPLES, CHUNK):
             picked = []
             for t in range(SLOTS):
                 column = (t * SAMPLES + first) // 16
-                picked.append(table_sb[:].indirect(offsets[:, column : column + width // 16]))
+                picked.append(table_sb[:].indirect(offsets[:, column : column + CHUNK // 16]))
 
-            faded0 = work.tile([P, width], F32, name="faded0")
-            nc.vector.tensor_tensor(faded0[:], picked[0], decay_older[:, :width], MULT)
-            if waiting is not None:
-                network(*waiting, is_last=False)
-            faded2 = work.tile([P, width], F32, name="faded2")
-            nc.vector.tensor_tensor(faded2[:], picked[2], decay_newer[:, :width], MULT)
-            older = work.tile([P, width], F32, name="older")
+            hid_ps = psum_hid.tile([P, CHUNK], F32, name="hid_ps")
+            nc.tensor.matmul(
+                hid_ps[:], w1_sb[:, 0, :], q_sb[:, first : first + CHUNK], start=True, stop=False
+            )
+
+            faded0 = work.tile([P, CHUNK], F32, name="faded0")
+            nc.vector.tensor_tensor(faded0[:], picked[0], decay_older[:], MULT)
+            faded2 = work.tile([P, CHUNK], F32, name="faded2")
+            nc.vector.tensor_tensor(faded2[:], picked[2], decay_newer[:], MULT)
+            older = work.tile([P, CHUNK], F32, name="older")
             nc.vector.tensor_tensor(older[:], picked[1], faded0[:], ADD)
-            newer = work.tile([P, width], F32, name="newer")
+            newer = work.tile([P, CHUNK], F32, name="newer")
             nc.vector.tensor_tensor(newer[:], picked[3], faded2[:], ADD)
-            waiting = (first, width, older, newer)
-            first += width
-        network(*waiting, is_last=True)
+            mem4 = work.tile([P, CHUNK], BF16, name="mem4")
+            nc.vector.scalar_tensor_tensor(mem4[:], older[:], WGT[1], newer[:], op0=MULT, op1=ADD)
+
+            nc.tensor.matmul(hid_ps[:], w1_mem[:], mem4[:], start=False, stop=True)
+            hid = work.tile([P, CHUNK], BF16, name="hid")
+            nc.scalar.activation(hid[:], hid_ps[:], RELU, bias=b1_sb[:, 0:1])
+
+            out_sb = work.tile([P, VBLOCKS, CHUNK], F32, name="out_sb")
+            for v in range(VBLOCKS):
+                out_ps = psum_out.tile([P, CHUNK], F32, name="out_ps")
+                nc.tensor.matmul(out_ps[:], w2_sb[:, v * P : (v + 1) * P], hid[:], start=True, stop=True)
+                nc.any.tensor_scalar_add(out_sb[:, v, :], out_ps[:], b2_sb[:, v : v + 1])
+                if v % 2 == 1:
+                    nc.sync.dma_start(
+                        out_blocks[:, v - 1 : v + 1, first : first + CHUNK], out_sb[:, v - 1 : v + 1, :]
+                    )

@@ -6,6 +6,7 @@ import concourse.mybir as mybir
 F32, BF16, U16 = mybir.dt.float32, mybir.dt.bfloat16, mybir.dt.uint16
 MULT, ADD = mybir.AluOpType.mult, mybir.AluOpType.add
 RELU = mybir.ActivationFunctionType.Relu
+IDENTITY = mybir.ActivationFunctionType.Identity
 
 P = 128
 WORDS = 512
@@ -82,7 +83,10 @@ def tile_ebbinghausmodel_kernel(tc, table, q, w1, b1, w2, b2, offs, out):
             for v in range(VBLOCKS):
                 out_ps = psum_out.tile([P, CHUNK], F32, name="out_ps")
                 nc.tensor.matmul(out_ps[:], w2_sb[:, v * P : (v + 1) * P], hid[:], start=True, stop=True)
-                nc.any.tensor_scalar_add(out_sb[:, v, :], out_ps[:], b2_sb[:, v : v + 1])
+                if first + CHUNK == SAMPLES and v % 2 == 0:
+                    nc.vector.tensor_scalar_add(out_sb[:, v, :], out_ps[:], b2_sb[:, v : v + 1])
+                else:
+                    nc.scalar.activation(out_sb[:, v, :], out_ps[:], IDENTITY, bias=b2_sb[:, v : v + 1])
                 if v % 2 == 1:
                     nc.sync.dma_start(
                         out_blocks[:, v - 1 : v + 1, first : first + CHUNK], out_sb[:, v - 1 : v + 1, :]

@@ -26,6 +26,7 @@ def tile_ebbinghausmodel_kernel(tc, table, q, w1, b1, w2, b2, offs, out):
     with ExitStack() as ctx:
         held = ctx.enter_context(tc.tile_pool(name="held", bufs=1))
         work = ctx.enter_context(tc.tile_pool(name="work", bufs=CHUNKS))
+        sums = ctx.enter_context(tc.tile_pool(name="sums", bufs=1))
         psum_hid = ctx.enter_context(tc.psum_pool(name="psum_hid", bufs=2))
         psum_out = ctx.enter_context(tc.psum_pool(name="psum_out", bufs=6))
 
@@ -64,13 +65,13 @@ def tile_ebbinghausmodel_kernel(tc, table, q, w1, b1, w2, b2, offs, out):
                 hid_ps[:], w1_sb[:, 0, :], q_sb[:, first : first + CHUNK], start=True, stop=False
             )
 
-            faded0 = work.tile([P, CHUNK], F32, name="faded0")
+            faded0 = sums.tile([P, CHUNK], F32, name="faded0")
             nc.vector.tensor_tensor(faded0[:], picked[0], decay_older[:], MULT)
-            faded2 = work.tile([P, CHUNK], F32, name="faded2")
+            faded2 = sums.tile([P, CHUNK], F32, name="faded2")
             nc.vector.tensor_tensor(faded2[:], picked[2], decay_newer[:], MULT)
-            older = work.tile([P, CHUNK], F32, name="older")
+            older = sums.tile([P, CHUNK], F32, name="older")
             nc.vector.tensor_tensor(older[:], picked[1], faded0[:], ADD)
-            newer = work.tile([P, CHUNK], F32, name="newer")
+            newer = sums.tile([P, CHUNK], F32, name="newer")
             nc.vector.tensor_tensor(newer[:], picked[3], faded2[:], ADD)
             mem4 = work.tile([P, CHUNK], BF16, name="mem4")
             nc.vector.scalar_tensor_tensor(mem4[:], older[:], WGT[1], newer[:], op0=MULT, op1=ADD)
@@ -83,7 +84,7 @@ def tile_ebbinghausmodel_kernel(tc, table, q, w1, b1, w2, b2, offs, out):
             for v in range(VBLOCKS):
                 out_ps = psum_out.tile([P, CHUNK], F32, name="out_ps")
                 nc.tensor.matmul(out_ps[:], w2_sb[:, v * P : (v + 1) * P], hid[:], start=True, stop=True)
-                if first + CHUNK == SAMPLES and v % 2 == 0:
+                if v == VBLOCKS - 1 or (first + CHUNK == SAMPLES and v % 2 == 1):
                     nc.vector.tensor_scalar_add(out_sb[:, v, :], out_ps[:], b2_sb[:, v : v + 1])
                 else:
                     nc.scalar.activation(out_sb[:, v, :], out_ps[:], IDENTITY, bias=b2_sb[:, v : v + 1])

@@ -54,6 +54,16 @@ def tile_ebbinghausmodel_kernel(tc, table, q, w1, b1, w2, b2, offs, out):
         w1_mem = held.tile([P, P], BF16, name="w1_mem")
         nc.scalar.mul(w1_mem[:], w1_sb[:, 1, :], 1.0 / SLOTS)
 
+        def add_bias_and_store(first, out_sb, out_ps, pair):
+            for v in pair:
+                if first + CHUNK == SAMPLES and v % 2 == 0:
+                    nc.vector.tensor_scalar_add(out_sb[:, v, :], out_ps[v][:], b2_sb[:, v : v + 1])
+                else:
+                    nc.scalar.activation(out_sb[:, v, :], out_ps[v][:], IDENTITY, bias=b2_sb[:, v : v + 1])
+            nc.sync.dma_start(
+                out_blocks[:, pair[0] : pair[1] + 1, first : first + CHUNK], out_sb[:, pair[0] : pair[1] + 1, :]
+            )
+
         for first in range(0, SAMPLES, CHUNK):
             picked = []
             for t in range(SLOTS):
@@ -80,15 +90,13 @@ def tile_ebbinghausmodel_kernel(tc, table, q, w1, b1, w2, b2, offs, out):
             hid = work.tile([P, CHUNK], BF16, name="hid")
             nc.scalar.activation(hid[:], hid_ps[:], RELU, bias=b1_sb[:, 0:1])
 
+            if first > 0:
+                add_bias_and_store(first - CHUNK, out_sb, out_ps, (2, 3))
+
             out_sb = work.tile([P, VBLOCKS, CHUNK], F32, name="out_sb")
+            out_ps = []
             for v in range(VBLOCKS):
-                out_ps = psum_out.tile([P, CHUNK], F32, name="out_ps")
-                nc.tensor.matmul(out_ps[:], w2_sb[:, v * P : (v + 1) * P], hid[:], start=True, stop=True)
-                if v == VBLOCKS - 1 or (first + CHUNK == SAMPLES and v % 2 == 1):
-                    nc.vector.tensor_scalar_add(out_sb[:, v, :], out_ps[:], b2_sb[:, v : v + 1])
-                else:
-                    nc.scalar.activation(out_sb[:, v, :], out_ps[:], IDENTITY, bias=b2_sb[:, v : v + 1])
-                if v % 2 == 1:
-                    nc.sync.dma_start(
-                        out_blocks[:, v - 1 : v + 1, first : first + CHUNK], out_sb[:, v - 1 : v + 1, :]
-                    )
+                out_ps.append(psum_out.tile([P, CHUNK], F32, name="out_ps"))
+                nc.tensor.matmul(out_ps[v][:], w2_sb[:, v * P : (v + 1) * P], hid[:], start=True, stop=True)
+            add_bias_and_store(first, out_sb, out_ps, (0, 1))
+        add_bias_and_store(SAMPLES - CHUNK, out_sb, out_ps, (2, 3))

@@ -15,8 +15,8 @@ SLOTS = 4
 VBLOCKS = 4
 WGT = [math.exp(-age * (age + 1) / 20.0) for age in (3, 2, 1, 0)]
 
-CHUNK = 128
-CHUNKS = SAMPLES // CHUNK
+WIDTHS = (192, 192, 128)
+assert sum(WIDTHS) == SAMPLES
 
 FLOPS = 2 * 256 * P * SAMPLES + 2 * P * 512 * SAMPLES
 
@@ -25,7 +25,7 @@ def tile_ebbinghausmodel_kernel(tc, table, q, w1, b1, w2, b2, offs, out):
     nc = tc.nc
     with ExitStack() as ctx:
         held = ctx.enter_context(tc.tile_pool(name="held", bufs=1))
-        work = ctx.enter_context(tc.tile_pool(name="work", bufs=CHUNKS))
+        work = ctx.enter_context(tc.tile_pool(name="work", bufs=len(WIDTHS)))
         sums = ctx.enter_context(tc.tile_pool(name="sums", bufs=1))
         psum_hid = ctx.enter_context(tc.psum_pool(name="psum_hid", bufs=2))
         psum_out = ctx.enter_context(tc.psum_pool(name="psum_out", bufs=6))
@@ -47,56 +47,59 @@ def tile_ebbinghausmodel_kernel(tc, table, q, w1, b1, w2, b2, offs, out):
             nc.sync.dma_start(b2_sb[:], b2.rearrange("(v p) one -> p (v one)", p=P))
         out_blocks = out.rearrange("(v p) n -> p v n", p=P)
 
-        decay_older = held.tile([P, CHUNK], F32, name="decay_older")
+        decay_older = held.tile([P, max(WIDTHS)], F32, name="decay_older")
         nc.gpsimd.memset(decay_older[:], WGT[0] / WGT[1])
-        decay_newer = held.tile([P, CHUNK], F32, name="decay_newer")
+        decay_newer = held.tile([P, max(WIDTHS)], F32, name="decay_newer")
         nc.gpsimd.memset(decay_newer[:], WGT[2])
         w1_mem = held.tile([P, P], BF16, name="w1_mem")
         nc.scalar.mul(w1_mem[:], w1_sb[:, 1, :], 1.0 / SLOTS)
 
-        def add_bias_and_store(first, out_sb, out_ps, pair):
+        def add_bias_and_store(first, width, out_sb, out_ps, pair):
             for v in pair:
-                if first + CHUNK == SAMPLES and v % 2 == 0:
+                if first + width == SAMPLES and v % 2 == 0:
                     nc.vector.tensor_scalar_add(out_sb[:, v, :], out_ps[v][:], b2_sb[:, v : v + 1])
                 else:
                     nc.scalar.activation(out_sb[:, v, :], out_ps[v][:], IDENTITY, bias=b2_sb[:, v : v + 1])
             nc.sync.dma_start(
-                out_blocks[:, pair[0] : pair[1] + 1, first : first + CHUNK], out_sb[:, pair[0] : pair[1] + 1, :]
+                out_blocks[:, pair[0] : pair[1] + 1, first : first + width], out_sb[:, pair[0] : pair[1] + 1, :]
             )
 
-        for first in range(0, SAMPLES, CHUNK):
+        first = 0
+        for width in WIDTHS:
             picked = []
             for t in range(SLOTS):
                 column = (t * SAMPLES + first) // 16
-                picked.append(table_sb[:].indirect(offsets[:, column : column + CHUNK // 16]))
+                picked.append(table_sb[:].indirect(offsets[:, column : column + width // 16]))
 
-            hid_ps = psum_hid.tile([P, CHUNK], F32, name="hid_ps")
+            hid_ps = psum_hid.tile([P, width], F32, name="hid_ps")
             nc.tensor.matmul(
-                hid_ps[:], w1_sb[:, 0, :], q_sb[:, first : first + CHUNK], start=True, stop=False
+                hid_ps[:], w1_sb[:, 0, :], q_sb[:, first : first + width], start=True, stop=False
             )
 
-            faded0 = sums.tile([P, CHUNK], F32, name="faded0")
-            nc.vector.tensor_tensor(faded0[:], picked[0], decay_older[:], MULT)
-            faded2 = sums.tile([P, CHUNK], F32, name="faded2")
-            nc.vector.tensor_tensor(faded2[:], picked[2], decay_newer[:], MULT)
-            older = sums.tile([P, CHUNK], F32, name="older")
+            faded0 = sums.tile([P, width], F32, name="faded0")
+            nc.vector.tensor_tensor(faded0[:], picked[0], decay_older[:, :width], MULT)
+            faded2 = sums.tile([P, width], F32, name="faded2")
+            nc.vector.tensor_tensor(faded2[:], picked[2], decay_newer[:, :width], MULT)
+            older = sums.tile([P, width], F32, name="older")
             nc.vector.tensor_tensor(older[:], picked[1], faded0[:], ADD)
-            newer = sums.tile([P, CHUNK], F32, name="newer")
+            newer = sums.tile([P, width], F32, name="newer")
             nc.vector.tensor_tensor(newer[:], picked[3], faded2[:], ADD)
-            mem4 = work.tile([P, CHUNK], BF16, name="mem4")
+            mem4 = work.tile([P, width], BF16, name="mem4")
             nc.vector.scalar_tensor_tensor(mem4[:], older[:], WGT[1], newer[:], op0=MULT, op1=ADD)
 
             nc.tensor.matmul(hid_ps[:], w1_mem[:], mem4[:], start=False, stop=True)
-            hid = work.tile([P, CHUNK], BF16, name="hid")
+            hid = work.tile([P, width], BF16, name="hid")
             nc.scalar.activation(hid[:], hid_ps[:], RELU, bias=b1_sb[:, 0:1])
 
             if first > 0:
-                add_bias_and_store(first - CHUNK, out_sb, out_ps, (2, 3))
+                add_bias_and_store(before[0], before[1], out_sb, out_ps, (2, 3))
 
-            out_sb = work.tile([P, VBLOCKS, CHUNK], F32, name="out_sb")
+            out_sb = work.tile([P, VBLOCKS, width], F32, name="out_sb")
             out_ps = []
             for v in range(VBLOCKS):
-                out_ps.append(psum_out.tile([P, CHUNK], F32, name="out_ps"))
+                out_ps.append(psum_out.tile([P, width], F32, name="out_ps"))
                 nc.tensor.matmul(out_ps[v][:], w2_sb[:, v * P : (v + 1) * P], hid[:], start=True, stop=True)
-            add_bias_and_store(first, out_sb, out_ps, (0, 1))
-        add_bias_and_store(SAMPLES - CHUNK, out_sb, out_ps, (2, 3))
+            add_bias_and_store(first, width, out_sb, out_ps, (0, 1))
+            before = (first, width)
+            first += width
+        add_bias_and_store(before[0], before[1], out_sb, out_ps, (2, 3))

@@ -48,9 +48,9 @@ def tile_ebbinghausmodel_kernel(tc, table, q, w1, b1, w2, b2, offs, out):
         out_blocks = out.rearrange("(v p) n -> p v n", p=P)
 
         decay_older = held.tile([P, max(WIDTHS)], F32, name="decay_older")
-        nc.gpsimd.memset(decay_older[:], WGT[0] / WGT[1])
+        nc.vector.memset(decay_older[:], WGT[0] / WGT[1])
         decay_newer = held.tile([P, max(WIDTHS)], F32, name="decay_newer")
-        nc.gpsimd.memset(decay_newer[:], WGT[2])
+        nc.vector.memset(decay_newer[:], WGT[2])
         w1_mem = held.tile([P, P], BF16, name="w1_mem")
         nc.scalar.mul(w1_mem[:], w1_sb[:, 1, :], 1.0 / SLOTS)
 

@@ -30,10 +30,10 @@ def tile_ebbinghausmodel_kernel(tc, table, q, w1, b1, w2, b2, offs, out):
         psum_hid = ctx.enter_context(tc.psum_pool(name="psum_hid", bufs=2))
         psum_out = ctx.enter_context(tc.psum_pool(name="psum_out", bufs=6))
 
-        offsets = held.tile([P, SLOTS * SAMPLES // 16], U16, name="offsets")
-        nc.sync.dma_start(offsets[:], offs)
         table_sb = held.tile([P, WORDS], F32, name="table_sb")
         nc.sync.dma_start(table_sb[:], table)
+        offsets = held.tile([P, SLOTS * SAMPLES // 16], U16, name="offsets")
+        nc.sync.dma_start(offsets[:], offs)
         w1_sb = held.tile([P, 2, P], BF16, name="w1_sb")
         nc.sync.dma_start(w1_sb[:], w1.rearrange("(half k) d -> k half d", k=P))
         q_sb = held.tile([P, SAMPLES], BF16, name="q_sb")

import math
from contextlib import ExitStack

import concourse.mybir as mybir

F32, BF16, U16 = mybir.dt.float32, mybir.dt.bfloat16, mybir.dt.uint16
MULT, ADD = mybir.AluOpType.mult, mybir.AluOpType.add
RELU = mybir.ActivationFunctionType.Relu
IDENTITY = mybir.ActivationFunctionType.Identity

P = 128
WORDS = 512
SAMPLES = 512
SLOTS = 4
VBLOCKS = 4
WGT = [math.exp(-age * (age + 1) / 20.0) for age in (3, 2, 1, 0)]

WIDTHS = (192, 192, 128)
assert sum(WIDTHS) == SAMPLES

FLOPS = 2 * 256 * P * SAMPLES + 2 * P * 512 * SAMPLES


def tile_ebbinghausmodel_kernel(tc, table, q, w1, b1, w2, b2, offs, out):
    nc = tc.nc
    with ExitStack() as ctx:
        held = ctx.enter_context(tc.tile_pool(name="held", bufs=1))
        work = ctx.enter_context(tc.tile_pool(name="work", bufs=len(WIDTHS)))
        sums = ctx.enter_context(tc.tile_pool(name="sums", bufs=1))
        psum_hid = ctx.enter_context(tc.psum_pool(name="psum_hid", bufs=2))
        psum_out = ctx.enter_context(tc.psum_pool(name="psum_out", bufs=6))

        table_sb = held.tile([P, WORDS], F32, name="table_sb")
        nc.sync.dma_start(table_sb[:], table)
        offsets = held.tile([P, SLOTS * SAMPLES // 16], U16, name="offsets")
        nc.sync.dma_start(offsets[:], offs)
        w1_sb = held.tile([P, 2, P], BF16, name="w1_sb")
        nc.sync.dma_start(w1_sb[:], w1.rearrange("(half k) d -> k half d", k=P))
        q_sb = held.tile([P, SAMPLES], BF16, name="q_sb")
        nc.sync.dma_start(q_sb[:], q)
        b1_sb = held.tile([P, 1], F32, name="b1_sb")
        nc.sync.dma_start(b1_sb[:], b1)
        w2_sb = held.tile([P, VBLOCKS * P], BF16, name="w2_sb")
        nc.sync.dma_start(w2_sb[:], w2)
        b2_sb = held.tile([P, VBLOCKS], F32, name="b2_sb")
        with nc.allow_non_contiguous_dma(reason="512 floats, one to a partition and block"):
            nc.sync.dma_start(b2_sb[:], b2.rearrange("(v p) one -> p (v one)", p=P))
        out_blocks = out.rearrange("(v p) n -> p v n", p=P)

        decay_older = held.tile([P, max(WIDTHS)], F32, name="decay_older")
        nc.vector.memset(decay_older[:], WGT[0] / WGT[1])
        decay_newer = held.tile([P, max(WIDTHS)], F32, name="decay_newer")
        nc.vector.memset(decay_newer[:], WGT[2])
        w1_mem = held.tile([P, P], BF16, name="w1_mem")
        nc.scalar.mul(w1_mem[:], w1_sb[:, 1, :], 1.0 / SLOTS)

        def add_bias_and_store(first, width, out_sb, out_ps, pair):
            for v in pair:
                if first + width == SAMPLES and v % 2 == 0:
                    nc.vector.tensor_scalar_add(out_sb[:, v, :], out_ps[v][:], b2_sb[:, v : v + 1])
                else:
                    nc.scalar.activation(out_sb[:, v, :], out_ps[v][:], IDENTITY, bias=b2_sb[:, v : v + 1])
            nc.sync.dma_start(
                out_blocks[:, pair[0] : pair[1] + 1, first : first + width], out_sb[:, pair[0] : pair[1] + 1, :]
            )

        first = 0
        for width in WIDTHS:
            picked = []
            for t in range(SLOTS):
                column = (t * SAMPLES + first) // 16
                picked.append(table_sb[:].indirect(offsets[:, column : column + width // 16]))

            hid_ps = psum_hid.tile([P, width], F32, name="hid_ps")
            nc.tensor.matmul(
                hid_ps[:], w1_sb[:, 0, :], q_sb[:, first : first + width], start=True, stop=False
            )

            faded0 = sums.tile([P, width], F32, name="faded0")
            nc.vector.tensor_tensor(faded0[:], picked[0], decay_older[:, :width], MULT)
            faded2 = sums.tile([P, width], F32, name="faded2")
            nc.vector.tensor_tensor(faded2[:], picked[2], decay_newer[:, :width], MULT)
            older = sums.tile([P, width], F32, name="older")
            nc.vector.tensor_tensor(older[:], picked[1], faded0[:], ADD)
            newer = sums.tile([P, width], F32, name="newer")
            nc.vector.tensor_tensor(newer[:], picked[3], faded2[:], ADD)
            mem4 = work.tile([P, width], BF16, name="mem4")
            nc.vector.scalar_tensor_tensor(mem4[:], older[:], WGT[1], newer[:], op0=MULT, op1=ADD)

            nc.tensor.matmul(hid_ps[:], w1_mem[:], mem4[:], start=False, stop=True)
            hid = work.tile([P, width], BF16, name="hid")
            nc.scalar.activation(hid[:], hid_ps[:], RELU, bias=b1_sb[:, 0:1])

            if first > 0:
                add_bias_and_store(before[0], before[1], out_sb, out_ps, (2, 3))

            out_sb = work.tile([P, VBLOCKS, width], F32, name="out_sb")
            out_ps = []
            for v in range(VBLOCKS):
                out_ps.append(psum_out.tile([P, width], F32, name="out_ps"))
                nc.tensor.matmul(out_ps[v][:], w2_sb[:, v * P : (v + 1) * P], hid[:], start=True, stop=True)
            add_bias_and_store(first, width, out_sb, out_ps, (0, 1))
            before = (first, width)
            first += width
        add_bias_and_store(before[0], before[1], out_sb, out_ps, (2, 3))
